import numpy as np
import ml_dtypes


def mxq(x, axis, fmt="e4m3"):
    dtype, down = {"e4m3": (ml_dtypes.float8_e4m3fn, 7), "e5m2": (ml_dtypes.float8_e5m2, 14)}[fmt]
    v = np.moveaxis(np.asarray(x, np.float32).astype(ml_dtypes.bfloat16).astype(np.float64), axis, -1)
    blocks = v.reshape(v.shape[:-1] + (-1, 32))
    amax = np.abs(blocks).max(-1, keepdims=True)
    byte = np.maximum(np.where(amax > 0, np.frexp(amax)[1] - 1 + 127, 0) - down, 1)
    scale = np.exp2(byte - 127.0)
    codes = (blocks / scale).astype(np.float32).astype(dtype).astype(np.float64)
    return np.moveaxis((codes * scale).reshape(v.shape), -1, axis)


WIDE = False


def mx_kscale(k):
    if not WIDE:
        return np.ones(k)
    levels = np.array([30, -30])
    if k % 512:
        return np.exp2(np.random.permutation(np.resize(levels, k // 32))).repeat(32)
    a = np.empty((k // 512, 16))
    for p in range(k // 512):
        a[p, :8] = np.random.permutation(np.resize(levels, 8))
        for g in range(8):
            far = levels[np.abs(levels - a[p, g]) >= 10]
            a[p, g + 8] = far[np.random.randint(len(far))]
    return np.exp2(a.ravel()).repeat(32)


BF16 = ml_dtypes.bfloat16


def bf(x):
    return np.asarray(x, np.float32).astype(BF16)


def f64(x):
    return np.asarray(x).astype(np.float64)


E2M1 = np.array([0.0, 0.5, 1.0, 1.5, 2.0, 3.0, 4.0, 6.0, -0.0, -0.5, -1.0, -1.5, -2.0, -3.0, -4.0, -6.0])


def pack_weight(w, fmt):
    k, n = w.shape
    w = f64(bf(w)).reshape(k // 32, 32, n)
    amax = np.abs(w).max(1)
    if fmt == "e4m3":
        byte = np.frexp(amax)[1] - 1 + 127 - 7
    else:
        mant, ex = np.frexp(amax / 6.0)
        byte = np.where(mant > 0.5, ex, ex - 1) + 127
    byte = np.clip(np.where(amax > 0, byte, 1), 1, 254)
    scaled = (w * np.exp2(127.0 - byte)[:, None, :]).reshape(k, n).astype(np.float32)
    by_word = np.ascontiguousarray(scaled.reshape(k // 512, 128, 4, n).transpose(0, 1, 3, 2))
    if fmt == "e4m3":
        words = by_word.astype(ml_dtypes.float8_e4m3fn).view(np.uint8)
    else:
        c = by_word.astype(ml_dtypes.float4_e2m1fn).view(np.uint8) & 0xF
        words = c[..., 0::2] | (c[..., 1::2] << 4)
    return np.ascontiguousarray(words), np.ascontiguousarray(byte.astype(np.uint8).reshape(k // 512, 16, n))


def unpack_weight(words, scales, fmt):
    g, p, n, _ = words.shape
    if fmt == "e4m3":
        vals = np.ascontiguousarray(words).view(ml_dtypes.float8_e4m3fn).astype(np.float64)
    else:
        nib = np.empty((g, p, n, 4), np.uint8)
        nib[..., 0::2] = words & 0xF
        nib[..., 1::2] = words >> 4
        vals = E2M1[nib]
    vals = vals * np.repeat(np.exp2(scales.astype(np.float64) - 127.0), 8, axis=1)[..., None]
    return vals.transpose(0, 1, 3, 2).reshape(g * 512, n)

def pack4(w):
    words, scales = pack_weight(w, "e2m1")
    return words.reshape(words.shape[0], 128, -1), scales


def unpack4(words, scales):
    return unpack_weight(words.reshape(words.shape[0], 128, -1, 2), scales, "e2m1")


B, S, HID, H, HK, D = 2, 256, 2048, 16, 4, 128
EPS = 1e-6
PRE = 0.004


def rmsnorm(v, w):
    var = np.mean(v * v, axis=-1, keepdims=True)
    return w * (v * (1.0 / np.sqrt(var + EPS)))


def rope(v, cos, sin):
    c = cos[:, :, None, :]
    sn = sin[:, :, None, :]
    v1, v2 = np.split(v, 2, axis=-1)
    rot = np.concatenate([-v2, v1], axis=-1)
    return v * c + rot * sn


def setup_inputs():
    s = mx_kscale(HID)
    hidden_states = bf(np.random.standard_normal((B, S, HID)) * s)
    cos = bf(np.cos(np.random.standard_normal((B, S, D))))
    sin = bf(np.sin(np.random.standard_normal((B, S, D))))
    wq = np.random.standard_normal((H * D, HID)) * PRE / np.sqrt(HID) / s
    wk = np.random.standard_normal((HK * D, HID)) * PRE / np.sqrt(HID) / s
    q_norm_w = bf(1.0 + 0.1 * np.random.standard_normal(D))
    k_norm_w = bf(1.0 + 0.1 * np.random.standard_normal(D))
    wq_words, wq_scales = pack4(np.ascontiguousarray(wq.T))
    wk_words, wk_scales = pack4(np.ascontiguousarray(wk.T))
    return {
        "hidden_states": hidden_states,
        "cos": cos,
        "sin": sin,
        "Wq_query_words": wq_words,
        "Wq_query_scales": wq_scales,
        "Wk_words": wk_words,
        "Wk_scales": wk_scales,
        "q_norm_w": q_norm_w,
        "k_norm_w": k_norm_w,
    }


def reference(hidden_states, cos, sin, Wq_query_words, Wq_query_scales, Wk_words, Wk_scales, q_norm_w, k_norm_w):
    xq = mxq(f64(hidden_states), 2, "e5m2")
    q = (xq @ unpack4(Wq_query_words, Wq_query_scales)).reshape(B, S, H, D)
    k = (xq @ unpack4(Wk_words, Wk_scales)).reshape(B, S, HK, D)
    q = rmsnorm(q, f64(q_norm_w))
    k = rmsnorm(k, f64(k_norm_w))
    q = rope(q, f64(cos), f64(sin))
    k = rope(k, f64(cos), f64(sin))
    return q, k

@@ -1,0 +1,220 @@
+from contextlib import ExitStack
+
+import concourse.mybir as mybir
+from concourse.masks import make_identity
+
+F32 = mybir.dt.float32
+BF16 = mybir.dt.bfloat16
+I32 = mybir.dt.int32
+U32 = mybir.dt.uint32
+U8 = mybir.dt.uint8
+E5M2X4 = mybir.dt.float8_e5m2_x4
+E2M1X4 = mybir.dt.float4_e2m1fn_x4
+ALU = mybir.AluOpType
+ACT = mybir.ActivationFunctionType
+
+P = 128
+TOKENS = 512
+HID = 2048
+D = 128
+HALF = D // 2
+EPS = 1e-6
+TILES = TOKENS // P
+PASSES = HID // 512
+BLOCK = 512
+HEADS = BLOCK // D
+Q_BLOCKS = 4
+BLOCKS = 1 + Q_BLOCKS
+LEAD = 3
+FLOPS = 2 * TOKENS * HID * BLOCKS * BLOCK
+
+
+def tile_qwen3nextattentionforengine_pa_kernel(
+    tc, hidden_states, cos, sin, wq_words, wq_scales, wk_words, wk_scales, q_norm_w, k_norm_w, out_0, out_1
+):
+    nc = tc.nc
+    x_dram = hidden_states.rearrange("b (q i) k -> (b q) i k", i=TILES)
+    cos_dram = cos.rearrange("b (q i) d -> (b q) i d", i=TILES)
+    sin_dram = sin.rearrange("b (q i) d -> (b q) i d", i=TILES)
+    q_dram = out_0.rearrange("b (q i) h d -> (b q) i (h d)", i=TILES)
+    k_dram = out_1.rearrange("b (q i) h d -> (b q) i (h d)", i=TILES)
+
+    with ExitStack() as ctx:
+        keep = ctx.enter_context(tc.tile_pool(name="keep", bufs=1))
+        work = ctx.enter_context(tc.tile_pool(name="work", bufs=3))
+        outs = ctx.enter_context(tc.tile_pool(name="outs", bufs=TILES * BLOCKS))
+        psum_t = ctx.enter_context(tc.psum_pool(name="psum_t", bufs=2))
+        psum_acc = ctx.enter_context(tc.psum_pool(name="psum_acc", bufs=6))
+        ctx.enter_context(tc.manual_schedule())
+
+        ident = keep.tile([P, P], F32, name="ident")
+        ones = keep.tile([P, P], BF16, name="ones")
+        w_rows = keep.tile([P, 2, D], BF16, name="w_rows")
+        cos_sb = keep.tile([P, TILES, D], BF16, name="cos_sb")
+        sin_sb = keep.tile([P, TILES, D], BF16, name="sin_sb")
+        x_sb = [[keep.tile([P, HID // 2], BF16, name="x%d_%d" % (i, hf)) for hf in range(2)] for i in range(TILES)]
+        x_codes = [keep.tile([P, PASSES, P], U32, name="xc%d" % i, align_bytes=64) for i in range(TILES)]
+        x_scales = [keep.tile([P, PASSES, P], U8, name="xs%d" % i, align_bytes=64) for i in range(TILES)]
+        w_words = [keep.tile([P, PASSES, 2 * BLOCK], U8, name="ww%d" % j, align_bytes=64) for j in range(BLOCKS)]
+        w_scales = [keep.tile([P, PASSES, BLOCK], U8, name="ws%d" % j, align_bytes=64) for j in range(BLOCKS)]
+        cos_tab = [keep.tile([P, TILES, D], F32, name="cos_tab%d" % kind) for kind in range(2)]
+        sin_tab = [keep.tile([P, TILES, D], F32, name="sin_tab%d" % kind) for kind in range(2)]
+
+        def load_x(i):
+            for hf in range(2):
+                nc.sync.dma_start(out=x_sb[i][hf][:], in_=x_dram[:, i, hf * (HID // 2) : (hf + 1) * (HID // 2)])
+
+        def load_w(j):
+            words, scales, c = (wk_words, wk_scales, 0) if j == 0 else (wq_words, wq_scales, j - 1)
+            for r in range(4):
+                nc.sync.dma_start(
+                    out=w_scales[j][r:P:32, :, :].bitcast(I32),
+                    in_=scales[:, r:16:4, c * BLOCK : (c + 1) * BLOCK].rearrange("g q n -> q g n").bitcast(I32),
+                )
+            nc.sync.dma_start(
+                out=w_words[j][:].bitcast(I32),
+                in_=words[:, :, 2 * c * BLOCK : 2 * (c + 1) * BLOCK].rearrange("g p n -> p g n").bitcast(I32),
+            )
+
+        grouped = {}
+
+        def transpose_x(i):
+            banks = []
+            for hf in range(2):
+                words = x_sb[i][hf][:].bitcast(F32)
+                xt = psum_t.tile([P, 2, 2, P], F32, name="xt")
+                for g in range(2):
+                    for u in range(2):
+                        nc.tensor.transpose(xt[:, g, u, :], words[:, 256 * g + u : 256 * (g + 1) : 2], ident[:])
+                banks.append(xt)
+            return banks
+
+        def copy_x(i, banks):
+            for hf in range(2):
+                xg = work.tile([P, HID // 2], BF16, name="xg", align_bytes=64)
+                nc.scalar.copy(
+                    out=xg[:].bitcast(F32).rearrange("p (g r u) -> p g r u", g=2, u=2),
+                    in_=banks[hf][:].rearrange("p g u r -> p g r u"),
+                )
+                grouped[(i, hf)] = xg
+
+        def quantize_x(i):
+            for hf in range(2):
+                nc.vector.quantize_mx(
+                    out=x_codes[i][:, 2 * hf : 2 * hf + 2, :].rearrange("p g r -> p (g r)").bitcast(E5M2X4),
+                    scales=x_scales[i][:, 2 * hf : 2 * hf + 2, :].rearrange("p g r -> p (g r)"),
+                    in_=grouped[(i, hf)][:],
+                )
+
+        def project(i, j):
+            acc = psum_acc.tile([P, BLOCK], F32, name="acc")
+            for g in range(PASSES):
+                nc.tensor.matmul_mx(
+                    out=acc[:],
+                    lhsT=x_codes[i][:, g, :].bitcast(E5M2X4),
+                    lhsT_scale=x_scales[i][:, g, :],
+                    rhs=w_words[j][:, g, :].bitcast(E2M1X4),
+                    rhs_scale=w_scales[j][:, g, :],
+                    start=(g == 0),
+                    stop=(g == PASSES - 1),
+                )
+            return acc
+
+        def inverse_rms(acc):
+            squares = work.tile([P, BLOCK], BF16, name="squares")
+            sums = work.tile([P, HEADS], F32, name="sums")
+            for h in range(HEADS):
+                nc.scalar.activation(
+                    out=squares[:, h * D : (h + 1) * D],
+                    in_=acc[:, h * D : (h + 1) * D],
+                    func=ACT.Square,
+                    accum_out=sums[:, h : h + 1],
+                )
+            rstd = work.tile([P, HEADS], F32, name="rstd")
+            nc.scalar.activation(out=rstd[:], in_=sums[:], func=ACT.Abs_reciprocal_sqrt, scale=1.0 / D, bias=EPS)
+            return rstd
+
+        def rotate(i, j, acc, rstd):
+            kind = min(j, 1)
+            straight = work.tile([P, BLOCK], F32, name="straight")
+            turned = work.tile([P, BLOCK], F32, name="turned")
+            for h in range(HEADS):
+                cols = slice(h * D, (h + 1) * D)
+                nc.vector.scalar_tensor_tensor(
+                    out=straight[:, cols],
+                    in0=acc[:, cols],
+                    scalar=rstd[:, h : h + 1],
+                    in1=cos_tab[kind][:, i, :],
+                    op0=ALU.mult,
+                    op1=ALU.mult,
+                )
+                nc.vector.scalar_tensor_tensor(
+                    out=turned[:, cols].rearrange("p (t e) -> p t e", t=2),
+                    in0=acc[:, cols].rearrange("p (t e) -> p t e", t=2)[:, ::-1, :],
+                    scalar=rstd[:, h : h + 1],
+                    in1=sin_tab[kind][:, i, :].rearrange("p (t e) -> p t e", t=2),
+                    op0=ALU.mult,
+                    op1=ALU.mult,
+                )
+            return straight, turned
+
+        def add_and_store(i, j, straight, turned):
+            result = outs.tile([P, BLOCK], F32, name="result")
+            nc.gpsimd.tensor_tensor(out=result[:], in0=straight[:], in1=turned[:], op=ALU.add)
+            dest = k_dram[:, i, :] if j == 0 else q_dram[:, i, (j - 1) * BLOCK : j * BLOCK]
+            nc.sync.dma_start(out=dest, in_=result[:])
+
+        make_identity(nc, ident[:])
+        nc.vector.memset(w_scales[0][:].bitcast(I32), 0)
+        nc.vector.memset(w_rows[:], 0.0)
+        nc.vector.memset(ones[:], 1.0)
+        for j in range(1, BLOCKS):
+            nc.vector.memset(w_scales[j][:].bitcast(I32), 0)
+        nc.gpsimd.dma_start(out=w_rows[0:1, 0, :], in_=k_norm_w.rearrange("(o d) -> o d", o=1))
+        nc.gpsimd.dma_start(out=w_rows[0:1, 1, :], in_=q_norm_w.rearrange("(o d) -> o d", o=1))
+
+        load_x(0)
+        load_w(0)
+        nc.sync.dma_start(out=cos_sb[:], in_=cos_dram)
+        nc.sync.dma_start(out=sin_sb[:], in_=sin_dram)
+        load_x(1)
+        for j in range(1, BLOCKS):
+            load_w(j)
+        for i in range(2, TILES):
+            load_x(i)
+
+        copy_x(0, transpose_x(0))
+        quantize_x(0)
+
+        w_all = psum_acc.tile([P, BLOCK], F32, name="acc")
+        nc.tensor.matmul(
+            w_all[:, 0 : 2 * D], lhsT=ones[:], rhs=w_rows[:].rearrange("p a d -> p (a d)"), start=True, stop=True
+        )
+        for kind in range(2):
+            w = w_all[:, kind * D : (kind + 1) * D]
+            nc.vector.tensor_tensor(
+                out=cos_tab[kind][:], in0=w.unsqueeze(1).to_broadcast([P, TILES, D]), in1=cos_sb[:], op=ALU.mult
+            )
+            for lo, other, sign in ((0, HALF, -1.0), (HALF, 0, 1.0)):
+                nc.vector.scalar_tensor_tensor(
+                    out=sin_tab[kind][:, :, lo : lo + HALF],
+                    in0=w[:, other : other + HALF].unsqueeze(1).to_broadcast([P, TILES, HALF]),
+                    scalar=sign,
+                    in1=sin_sb[:, :, lo : lo + HALF],
+                    op0=ALU.mult,
+                    op1=ALU.mult,
+                )
+
+        order = [(i, j) for i in range(2) for j in range(2)]
+        order += [(i, j) for j in range(2, BLOCKS) for i in range(2)]
+        order += [(i, j) for i in range(2, TILES) for j in range(BLOCKS)]
+        prepare_at = {max(0, order.index((i, 0)) - LEAD): i for i in range(1, TILES)}
+        for n, (i, j) in enumerate(order):
+            acc = project(i, j)
+            rstd = inverse_rms(acc)
+            if n in prepare_at:
+                copy_x(prepare_at[n], transpose_x(prepare_at[n]))
+            straight, turned = rotate(i, j, acc, rstd)
+            if n in prepare_at:
+                quantize_x(prepare_at[n])
+            add_and_store(i, j, straight, turned)

@@ -142,25 +142,25 @@ def tile_qwen3nextattentionforengine_pa_kernel(
                 cols = slice(h * D, (h + 1) * D)
                 nc.vector.scalar_tensor_tensor(
                     out=straight[:, cols],
-                    in0=acc[:, cols],
+                    in0=cos_tab[kind][:, i, :],
                     scalar=rstd[:, h : h + 1],
-                    in1=cos_tab[kind][:, i, :],
+                    in1=acc[:, cols],
                     op0=ALU.mult,
                     op1=ALU.mult,
                 )
                 nc.vector.scalar_tensor_tensor(
                     out=turned[:, cols].rearrange("p (t e) -> p t e", t=2),
-                    in0=acc[:, cols].rearrange("p (t e) -> p t e", t=2)[:, ::-1, :],
+                    in0=sin_tab[kind][:, i, :].rearrange("p (t e) -> p t e", t=2),
                     scalar=rstd[:, h : h + 1],
-                    in1=sin_tab[kind][:, i, :].rearrange("p (t e) -> p t e", t=2),
+                    in1=acc[:, cols].rearrange("p (t e) -> p t e", t=2)[:, ::-1, :],
                     op0=ALU.mult,
                     op1=ALU.mult,
                 )
             return straight, turned
 
-        def add_and_store(i, j, straight, turned):
+        def add_and_store(i, j, straight, turned, engine):
             result = outs.tile([P, BLOCK], F32, name="result")
-            nc.gpsimd.tensor_tensor(out=result[:], in0=straight[:], in1=turned[:], op=ALU.add)
+            engine.tensor_tensor(out=result[:], in0=straight[:], in1=turned[:], op=ALU.add)
             dest = k_dram[:, i, :] if j == 0 else q_dram[:, i, (j - 1) * BLOCK : j * BLOCK]
             nc.sync.dma_start(out=dest, in_=result[:])
 
@@ -217,4 +217,4 @@ def tile_qwen3nextattentionforengine_pa_kernel(
             straight, turned = rotate(i, j, acc, rstd)
             if n in prepare_at:
                 quantize_x(prepare_at[n])
-            add_and_store(i, j, straight, turned)
+            add_and_store(i, j, straight, turned, nc.vector if n == len(order) - 1 else nc.gpsimd)

from contextlib import ExitStack

import concourse.mybir as mybir
from concourse.masks import make_identity

F32 = mybir.dt.float32
BF16 = mybir.dt.bfloat16
I32 = mybir.dt.int32
U32 = mybir.dt.uint32
U8 = mybir.dt.uint8
E5M2X4 = mybir.dt.float8_e5m2_x4
E2M1X4 = mybir.dt.float4_e2m1fn_x4
ALU = mybir.AluOpType
ACT = mybir.ActivationFunctionType

P = 128
TOKENS = 512
HID = 2048
D = 128
HALF = D // 2
EPS = 1e-6
TILES = TOKENS // P
PASSES = HID // 512
BLOCK = 512
HEADS = BLOCK // D
Q_BLOCKS = 4
BLOCKS = 1 + Q_BLOCKS
LEAD = 3
FLOPS = 2 * TOKENS * HID * BLOCKS * BLOCK


def tile_qwen3nextattentionforengine_pa_kernel(
    tc, hidden_states, cos, sin, wq_words, wq_scales, wk_words, wk_scales, q_norm_w, k_norm_w, out_0, out_1
):
    nc = tc.nc
    x_dram = hidden_states.rearrange("b (q i) k -> (b q) i k", i=TILES)
    cos_dram = cos.rearrange("b (q i) d -> (b q) i d", i=TILES)
    sin_dram = sin.rearrange("b (q i) d -> (b q) i d", i=TILES)
    q_dram = out_0.rearrange("b (q i) h d -> (b q) i (h d)", i=TILES)
    k_dram = out_1.rearrange("b (q i) h d -> (b q) i (h d)", i=TILES)

    with ExitStack() as ctx:
        keep = ctx.enter_context(tc.tile_pool(name="keep", bufs=1))
        work = ctx.enter_context(tc.tile_pool(name="work", bufs=3))
        outs = ctx.enter_context(tc.tile_pool(name="outs", bufs=TILES * BLOCKS))
        psum_t = ctx.enter_context(tc.psum_pool(name="psum_t", bufs=2))
        psum_acc = ctx.enter_context(tc.psum_pool(name="psum_acc", bufs=6))
        ctx.enter_context(tc.manual_schedule())

        ident = keep.tile([P, P], F32, name="ident")
        ones = keep.tile([P, P], BF16, name="ones")
        w_rows = keep.tile([P, 2, D], BF16, name="w_rows")
        cos_sb = keep.tile([P, TILES, D], BF16, name="cos_sb")
        sin_sb = keep.tile([P, TILES, D], BF16, name="sin_sb")
        x_sb = [[keep.tile([P, HID // 2], BF16, name="x%d_%d" % (i, hf)) for hf in range(2)] for i in range(TILES)]
        x_codes = [keep.tile([P, PASSES, P], U32, name="xc%d" % i, align_bytes=64) for i in range(TILES)]
        x_scales = [keep.tile([P, PASSES, P], U8, name="xs%d" % i, align_bytes=64) for i in range(TILES)]
        w_words = [keep.tile([P, PASSES, 2 * BLOCK], U8, name="ww%d" % j, align_bytes=64) for j in range(BLOCKS)]
        w_scales = [keep.tile([P, PASSES, BLOCK], U8, name="ws%d" % j, align_bytes=64) for j in range(BLOCKS)]
        cos_tab = [keep.tile([P, TILES, D], F32, name="cos_tab%d" % kind) for kind in range(2)]
        sin_tab = [keep.tile([P, TILES, D], F32, name="sin_tab%d" % kind) for kind in range(2)]

        def load_x(i):
            for hf in range(2):
                nc.sync.dma_start(out=x_sb[i][hf][:], in_=x_dram[:, i, hf * (HID // 2) : (hf + 1) * (HID // 2)])

        def load_w(j):
            words, scales, c = (wk_words, wk_scales, 0) if j == 0 else (wq_words, wq_scales, j - 1)
            for r in range(4):
                nc.sync.dma_start(
                    out=w_scales[j][r:P:32, :, :].bitcast(I32),
                    in_=scales[:, r:16:4, c * BLOCK : (c + 1) * BLOCK].rearrange("g q n -> q g n").bitcast(I32),
                )
            nc.sync.dma_start(
                out=w_words[j][:].bitcast(I32),
                in_=words[:, :, 2 * c * BLOCK : 2 * (c + 1) * BLOCK].rearrange("g p n -> p g n").bitcast(I32),
            )

        grouped = {}

        def transpose_x(i):
            banks = []
            for hf in range(2):
                words = x_sb[i][hf][:].bitcast(F32)
                xt = psum_t.tile([P, 2, 2, P], F32, name="xt")
                for g in range(2):
                    for u in range(2):
                        nc.tensor.transpose(xt[:, g, u, :], words[:, 256 * g + u : 256 * (g + 1) : 2], ident[:])
                banks.append(xt)
            return banks

        def copy_x(i, banks):
            for hf in range(2):
                xg = work.tile([P, HID // 2], BF16, name="xg", align_bytes=64)
                nc.scalar.copy(
                    out=xg[:].bitcast(F32).rearrange("p (g r u) -> p g r u", g=2, u=2),
                    in_=banks[hf][:].rearrange("p g u r -> p g r u"),
                )
                grouped[(i, hf)] = xg

        def quantize_x(i):
            for hf in range(2):
                nc.vector.quantize_mx(
                    out=x_codes[i][:, 2 * hf : 2 * hf + 2, :].rearrange("p g r -> p (g r)").bitcast(E5M2X4),
                    scales=x_scales[i][:, 2 * hf : 2 * hf + 2, :].rearrange("p g r -> p (g r)"),
                    in_=grouped[(i, hf)][:],
                )

        def project(i, j):
            acc = psum_acc.tile([P, BLOCK], F32, name="acc")
            for g in range(PASSES):
                nc.tensor.matmul_mx(
                    out=acc[:],
                    lhsT=x_codes[i][:, g, :].bitcast(E5M2X4),
                    lhsT_scale=x_scales[i][:, g, :],
                    rhs=w_words[j][:, g, :].bitcast(E2M1X4),
                    rhs_scale=w_scales[j][:, g, :],
                    start=(g == 0),
                    stop=(g == PASSES - 1),
                )
            return acc

        def inverse_rms(acc):
            squares = work.tile([P, BLOCK], BF16, name="squares")
            sums = work.tile([P, HEADS], F32, name="sums")
            for h in range(HEADS):
                nc.scalar.activation(
                    out=squares[:, h * D : (h + 1) * D],
                    in_=acc[:, h * D : (h + 1) * D],
                    func=ACT.Square,
                    accum_out=sums[:, h : h + 1],
                )
            rstd = work.tile([P, HEADS], F32, name="rstd")
            nc.scalar.activation(out=rstd[:], in_=sums[:], func=ACT.Abs_reciprocal_sqrt, scale=1.0 / D, bias=EPS)
            return rstd

        def rotate(i, j, acc, rstd):
            kind = min(j, 1)
            straight = work.tile([P, BLOCK], F32, name="straight")
            turned = work.tile([P, BLOCK], F32, name="turned")
            for h in range(HEADS):
                cols = slice(h * D, (h + 1) * D)
                nc.vector.scalar_tensor_tensor(
                    out=straight[:, cols],
                    in0=cos_tab[kind][:, i, :],
                    scalar=rstd[:, h : h + 1],
                    in1=acc[:, cols],
                    op0=ALU.mult,
                    op1=ALU.mult,
                )
                nc.vector.scalar_tensor_tensor(
                    out=turned[:, cols].rearrange("p (t e) -> p t e", t=2),
                    in0=sin_tab[kind][:, i, :].rearrange("p (t e) -> p t e", t=2),
                    scalar=rstd[:, h : h + 1],
                    in1=acc[:, cols].rearrange("p (t e) -> p t e", t=2)[:, ::-1, :],
                    op0=ALU.mult,
                    op1=ALU.mult,
                )
            return straight, turned

        def add_and_store(i, j, straight, turned, engine):
            result = outs.tile([P, BLOCK], F32, name="result")
            engine.tensor_tensor(out=result[:], in0=straight[:], in1=turned[:], op=ALU.add)
            dest = k_dram[:, i, :] if j == 0 else q_dram[:, i, (j - 1) * BLOCK : j * BLOCK]
            nc.sync.dma_start(out=dest, in_=result[:])

        make_identity(nc, ident[:])
        nc.vector.memset(w_scales[0][:].bitcast(I32), 0)
        nc.vector.memset(w_rows[:], 0.0)
        nc.vector.memset(ones[:], 1.0)
        for j in range(1, BLOCKS):
            nc.vector.memset(w_scales[j][:].bitcast(I32), 0)
        nc.gpsimd.dma_start(out=w_rows[0:1, 0, :], in_=k_norm_w.rearrange("(o d) -> o d", o=1))
        nc.gpsimd.dma_start(out=w_rows[0:1, 1, :], in_=q_norm_w.rearrange("(o d) -> o d", o=1))

        load_x(0)
        load_w(0)
        nc.sync.dma_start(out=cos_sb[:], in_=cos_dram)
        nc.sync.dma_start(out=sin_sb[:], in_=sin_dram)
        load_x(1)
        for j in range(1, BLOCKS):
            load_w(j)
        for i in range(2, TILES):
            load_x(i)

        copy_x(0, transpose_x(0))
        quantize_x(0)

        w_all = psum_acc.tile([P, BLOCK], F32, name="acc")
        nc.tensor.matmul(
            w_all[:, 0 : 2 * D], lhsT=ones[:], rhs=w_rows[:].rearrange("p a d -> p (a d)"), start=True, stop=True
        )
        for kind in range(2):
            w = w_all[:, kind * D : (kind + 1) * D]
            nc.vector.tensor_tensor(
                out=cos_tab[kind][:], in0=w.unsqueeze(1).to_broadcast([P, TILES, D]), in1=cos_sb[:], op=ALU.mult
            )
            for lo, other, sign in ((0, HALF, -1.0), (HALF, 0, 1.0)):
                nc.vector.scalar_tensor_tensor(
                    out=sin_tab[kind][:, :, lo : lo + HALF],
                    in0=w[:, other : other + HALF].unsqueeze(1).to_broadcast([P, TILES, HALF]),
                    scalar=sign,
                    in1=sin_sb[:, :, lo : lo + HALF],
                    op0=ALU.mult,
                    op1=ALU.mult,
                )

        order = [(i, j) for i in range(2) for j in range(2)]
        order += [(i, j) for j in range(2, BLOCKS) for i in range(2)]
        order += [(i, j) for i in range(2, TILES) for j in range(BLOCKS)]
        prepare_at = {max(0, order.index((i, 0)) - LEAD): i for i in range(1, TILES)}
        for n, (i, j) in enumerate(order):
            acc = project(i, j)
            rstd = inverse_rms(acc)
            if n in prepare_at:
                copy_x(prepare_at[n], transpose_x(prepare_at[n]))
            straight, turned = rotate(i, j, acc, rstd)
            if n in prepare_at:
                quantize_x(prepare_at[n])
            add_and_store(i, j, straight, turned, nc.vector if n == len(order) - 1 else nc.gpsimd)
